import numpy as np
import ml_dtypes


def mxq(x, axis, fmt="e4m3"):
    dtype, down = {"e4m3": (ml_dtypes.float8_e4m3fn, 7), "e5m2": (ml_dtypes.float8_e5m2, 14)}[fmt]
    v = np.moveaxis(np.asarray(x, np.float32).astype(ml_dtypes.bfloat16).astype(np.float64), axis, -1)
    blocks = v.reshape(v.shape[:-1] + (-1, 32))
    amax = np.abs(blocks).max(-1, keepdims=True)
    byte = np.maximum(np.where(amax > 0, np.frexp(amax)[1] - 1 + 127, 0) - down, 1)
    scale = np.exp2(byte - 127.0)
    codes = (blocks / scale).astype(np.float32).astype(dtype).astype(np.float64)
    return np.moveaxis((codes * scale).reshape(v.shape), -1, axis)


WIDE = False


def mx_kscale(k):
    if not WIDE:
        return np.ones(k)
    levels = np.array([10, -10, 5, -5, 0])
    a = np.random.permutation(np.resize(levels, k // 512 * 4)).reshape(k // 512, 4)
    idx = np.arange(k)
    return np.exp2(a[idx // 512, idx % 128 // 32])


BF16 = ml_dtypes.bfloat16


def bf(x):
    return np.asarray(x, np.float32).astype(BF16)


def f64(x):
    return np.asarray(x).astype(np.float64)


B, CIN, CM, CO, H, WD = 1, 512, 512, 512, 16, 16
RING = [(-1, -1), (-1, 0), (-1, 1), (0, 1), (1, 1), (1, 0), (1, -1), (0, -1)]
NUM_K = 9
KERNEL_ROT = 4
STEP = 2
M = NUM_K * CM


def setup_inputs():
    s = mx_kscale(CIN)
    t = mx_kscale(CM)
    return {"x": bf(np.random.standard_normal((B, CIN, H, WD)) * s[None, :, None, None]),
            "W": bf(np.random.standard_normal((CM, CIN, NUM_K)) / np.sqrt(CIN) / s[None, :, None] * t[:, None, None]),
            "W1": bf(np.random.standard_normal((CO, M)) * 1.4 / np.sqrt(M) / np.tile(t, NUM_K)[None, :])}


def reference(x, W, W1):
    xq = mxq(f64(x), 1, "e4m3")
    Wq = mxq(f64(W), 1, "e4m3")
    z = (Wq.transpose(0, 2, 1).reshape(CM * NUM_K, CIN) @ xq.reshape(B, CIN, H * WD)).reshape(B, CM, NUM_K, H, WD)
    h = np.maximum(z, 0.0)
    hq = mxq(h, 1, "e4m3")
    W1q = mxq(f64(W1).reshape(CO, NUM_K, CM), 2, "e4m3")
    u = (W1q.transpose(1, 0, 2) @ hq.transpose(0, 2, 1, 3, 4).reshape(B, NUM_K, CM, H * WD)).reshape(B, NUM_K, CO, H, WD)
    up = np.pad(u, ((0, 0), (0, 0), (0, 0), (1, 1), (1, 1)))
    rot_out = []
    for rot in range(KERNEL_ROT):
        roff = STEP * rot
        acc = 0.0
        for k in range(NUM_K):
            dy, dx = (0, 0) if k == NUM_K - 1 else RING[(k + roff) % len(RING)]
            acc = acc + up[:, k, :, 1 + dy:1 + dy + H, 1 + dx:1 + dx + WD]
        rot_out.append(acc)
    return np.stack(rot_out, axis=2)

@@ -1,0 +1,209 @@
+from contextlib import ExitStack
+
+import concourse.masks as masks
+import concourse.mybir as mybir
+
+BF16 = mybir.dt.bfloat16
+F32 = mybir.dt.float32
+U32 = mybir.dt.uint32
+U8 = mybir.dt.uint8
+FP8X4 = mybir.dt.float8_e4m3fn_x4
+RELU = mybir.ActivationFunctionType.Relu
+
+P = 128
+PACK = 4
+CH = 512
+TILES = CH // P
+NUM_K = 9
+CENTRE = 8
+SIDE = 16
+PIXELS = SIDE * SIDE
+ROTATIONS = 4
+RING = [(-1, -1), (-1, 0), (-1, 1), (0, 1), (1, 1), (1, 0), (1, -1), (0, -1)]
+PLANES = 3
+
+FLOPS = 2 * 2 * NUM_K * CH * CH * PIXELS
+
+
+def shift_of(k, r):
+    return (0, 0) if k == CENTRE else RING[(k + 2 * r) % len(RING)]
+
+
+def tile_psr4convf_kernel(tc, x, W, W1, out):
+    nc = tc.nc
+    with ExitStack() as ctx:
+        keep = ctx.enter_context(tc.tile_pool(name="keep", bufs=1))
+        w_in = ctx.enter_context(tc.tile_pool(name="w_in", bufs=TILES))
+        w1_in = ctx.enter_context(tc.tile_pool(name="w1_in", bufs=7))
+        stage = ctx.enter_context(tc.tile_pool(name="stage", bufs=4))
+        work = ctx.enter_context(tc.psum_pool(name="work", bufs=4))
+        sums = ctx.enter_context(tc.psum_pool(name="sums", bufs=4))
+
+        x_rows = keep.tile([P, PACK, PIXELS], BF16)
+        nc.sync.dma_start(
+            out=x_rows[:].rearrange("q (u e) n -> q u e n", u=2),
+            in_=x[0].rearrange("(u q e) h w -> q u e (h w)", u=2, e=2),
+        )
+        w_dram = W.rearrange("(u q e) c k -> u e q (c k)", u=2, e=2)
+        w_rows = []
+        for t in range(TILES):
+            rows = w_in.tile([P, CH * NUM_K], BF16, name="w_rows")
+            nc.sync.dma_start(out=rows[:], in_=w_dram[t // 2, t % 2])
+            w_rows.append(rows)
+        w1_dram = W1.rearrange("(a q) (k o) -> k q a o", q=P, k=NUM_K)
+        w1_rows = []
+        for k in range(NUM_K):
+            rows = w1_in.tile([P, TILES * CH], BF16, name="w1_rows")
+            nc.sync.dma_start(out=rows[:].rearrange("q (a o) -> q a o", a=TILES), in_=w1_dram[k])
+            w1_rows.append(rows)
+
+        ident = keep.tile([P, P], F32)
+        masks.make_identity(nc, ident[:])
+        padded = (SIDE + 2) * SIDE * PACK
+        h_image = {}
+        for dx in (-1, 0, 1):
+            for slot in range(2):
+                image = keep.tile([P, padded], BF16, align_bytes=64, name="h_image_%d_%d" % (dx + 1, slot))
+                nc.vector.memset(image[:], 0.0)
+                h_image[(dx, slot)] = image
+
+        x_grouped = keep.tile([P, PIXELS, PACK], BF16, align_bytes=64)
+        x_codes = keep.tile([P, PIXELS], U32, align_bytes=64)
+        x_scales = keep.tile([P, PIXELS], U8, align_bytes=64)
+        nc.vector.tensor_copy(out=x_grouped[:], in_=x_rows[:].rearrange("q t n -> q n t"))
+        nc.vector.quantize_mx(
+            out=x_codes[:].bitcast(FP8X4),
+            scales=x_scales[:],
+            in_=x_grouped[:].rearrange("q n t -> q (n t)"),
+        )
+
+        def transpose_and_quantise(first, second, codes, scales):
+            bank = work.tile([P, 2, 2, P], F32, tag="work", name="bank")
+            for a, words in enumerate((first, second)):
+                for u in range(2):
+                    nc.tensor.transpose(bank[:, a, u, :], words[:, u * P : (u + 1) * P], ident[:])
+            grouped = stage.tile([P, 2 * P * PACK], BF16, align_bytes=64, name="grouped")
+            nc.scalar.copy(
+                out=grouped[:].bitcast(F32).rearrange("q (a c u) -> q a c u", a=2, u=2),
+                in_=bank[:].rearrange("q a u c -> q a c u"),
+            )
+            nc.vector.quantize_mx(out=codes.bitcast(FP8X4), scales=scales, in_=grouped[:])
+
+        w_by_k = []
+        for t in range(TILES):
+            planes = keep.tile([P, NUM_K * CH], BF16, name="w_by_k%d" % t)
+            for g in range(NUM_K // PLANES):
+                ks = slice(g * PLANES, (g + 1) * PLANES)
+                src = w_rows[t][:].rearrange("q (c k) -> q c k", k=NUM_K)[:, :, ks]
+                dst = planes[:].rearrange("q (k c) -> q c k", k=NUM_K)[:, :, ks]
+                if g < 2:
+                    nc.vector.tensor_copy(out=dst, in_=src)
+                else:
+                    nc.scalar.copy(out=dst, in_=src)
+            w_by_k.append(planes)
+
+        w_codes = keep.tile([P, TILES // 2, NUM_K, 2 * P], U32, align_bytes=64)
+        w_scales = keep.tile([P, TILES // 2, NUM_K, 2 * P], U8, align_bytes=64)
+        w1_codes = keep.tile([P, TILES // 2, NUM_K, 2 * P], U32, align_bytes=64)
+        w1_scales = keep.tile([P, TILES // 2, NUM_K, 2 * P], U8, align_bytes=64)
+        words_of_k = CH // 2
+        for pair in range(TILES // 2):
+            for k in range(NUM_K):
+                cols = slice(k * words_of_k, (k + 1) * words_of_k)
+                transpose_and_quantise(
+                    w_by_k[2 * pair][:].bitcast(F32)[:, cols],
+                    w_by_k[2 * pair + 1][:].bitcast(F32)[:, cols],
+                    w_codes[:, pair, k, :],
+                    w_scales[:, pair, k, :],
+                )
+
+        h_codes = keep.tile([P, NUM_K, ROTATIONS // 2, 2 * PIXELS], U32, align_bytes=64)
+        h_scales = keep.tile([P, NUM_K, ROTATIONS // 2, 2 * PIXELS], U8, align_bytes=64)
+
+        def hidden_layer(k):
+            slot = k % 2
+            centred = h_image[(0, slot)]
+            half_pixels = PIXELS // 2
+            for half in range(2):
+                z = work.tile([P, PACK, half_pixels], F32, tag="work", name="z")
+                pixels = slice(half * half_pixels, (half + 1) * half_pixels)
+                for t in range(TILES):
+                    cols = slice((t % 2) * P, (t % 2 + 1) * P)
+                    nc.tensor.matmul_mx(
+                        out=z[:, t, :],
+                        lhsT=w_codes[:, t // 2, k, cols].bitcast(FP8X4),
+                        lhsT_scale=w_scales[:, t // 2, k, cols],
+                        rhs=x_codes[:, pixels].bitcast(FP8X4),
+                        rhs_scale=x_scales[:, pixels],
+                        start=True,
+                        stop=True,
+                    )
+                begin = (SIDE + half * half_pixels) * PACK
+                nc.scalar.activation(
+                    out=centred[:, begin : begin + half_pixels * PACK].rearrange("q (n t) -> q n t", t=PACK),
+                    in_=z[:].rearrange("q t n -> q n t"),
+                    func=RELU,
+                )
+            rotations = ROTATIONS // 2 if k == CENTRE else ROTATIONS
+            shifts = [shift_of(k, r) for r in range(rotations)]
+            for dx in (-1, 1):
+                if any(s[1] == dx for s in shifts):
+                    lo, hi = max(0, -dx), SIDE - max(0, dx)
+                    src = centred[:].rearrange("q (i j t) -> q i j t", j=SIDE, t=PACK)
+                    dst = h_image[(dx, slot)][:].rearrange("q (i j t) -> q i j t", j=SIDE, t=PACK)
+                    nc.vector.tensor_copy(
+                        out=dst[:, 1 : SIDE + 1, lo:hi, :], in_=src[:, 1 : SIDE + 1, lo + dx : hi + dx, :]
+                    )
+            for r, (dy, dx) in enumerate(shifts):
+                begin = (1 + dy) * SIDE * PACK
+                cols = slice((r % 2) * PIXELS, (r % 2 + 1) * PIXELS)
+                nc.vector.quantize_mx(
+                    out=h_codes[:, k, r // 2, cols].bitcast(FP8X4),
+                    scales=h_scales[:, k, r // 2, cols],
+                    in_=h_image[(dx, slot)][:, begin : begin + PIXELS * PACK],
+                )
+
+        def add_position(total, a, k, pair):
+            cols = slice((a % 2) * P, (a % 2 + 1) * P)
+            h_pair = 0 if k == CENTRE else pair
+            nc.tensor.matmul_mx(
+                out=total[:],
+                lhsT=w1_codes[:, a // 2, k, cols].bitcast(FP8X4),
+                lhsT_scale=w1_scales[:, a // 2, k, cols],
+                rhs=h_codes[:, k, h_pair, :].bitcast(FP8X4),
+                rhs_scale=h_scales[:, k, h_pair, :],
+                start=(k == 0),
+                stop=(k == NUM_K - 1),
+            )
+
+        out_dram = out[0].rearrange("(a q) (s r) h w -> a s q (r h w)", q=P, s=2)
+
+        def store(total, a, pair):
+            result = stage.tile([P, 2 * PIXELS], F32, name="result")
+            nc.scalar.copy(out=result[:], in_=total[:])
+            nc.sync.dma_start(out=out_dram[a, pair], in_=result[:])
+
+        totals = []
+        for a in range(TILES):
+            total = sums.tile([P, 2 * PIXELS], F32, tag="sums", name="total")
+            totals.append(total)
+        for k in range(NUM_K):
+            for pair in range(TILES // 2):
+                words = w1_rows[k][:].bitcast(F32)
+                transpose_and_quantise(
+                    words[:, 2 * pair * words_of_k : (2 * pair + 1) * words_of_k],
+                    words[:, (2 * pair + 1) * words_of_k : (2 * pair + 2) * words_of_k],
+                    w1_codes[:, pair, k, :],
+                    w1_scales[:, pair, k, :],
+                )
+            hidden_layer(k)
+            for a in range(TILES):
+                add_position(totals[a], a, k, 0)
+        for a in range(TILES):
+            store(totals[a], a, 0)
+
+        for a in range(TILES):
+            total = sums.tile([P, 2 * PIXELS], F32, tag="sums", name="total")
+            for k in range(NUM_K):
+                add_position(total, a, k, 1)
+            store(total, a, 1)

@@ -21,6 +21,8 @@ PIXELS = SIDE * SIDE
 ROTATIONS = 4
 RING = [(-1, -1), (-1, 0), (-1, 1), (0, 1), (1, 1), (1, 0), (1, -1), (0, -1)]
 PLANES = 3
+BANKS = 8
+WORK_BANKS = (6, 7)
 
 FLOPS = 2 * 2 * NUM_K * CH * CH * PIXELS
 
@@ -36,8 +38,10 @@ def tile_psr4convf_kernel(tc, x, W, W1, out):
         w_in = ctx.enter_context(tc.tile_pool(name="w_in", bufs=TILES))
         w1_in = ctx.enter_context(tc.tile_pool(name="w1_in", bufs=7))
         stage = ctx.enter_context(tc.tile_pool(name="stage", bufs=4))
-        work = ctx.enter_context(tc.psum_pool(name="work", bufs=4))
-        sums = ctx.enter_context(tc.psum_pool(name="sums", bufs=4))
+        psum = ctx.enter_context(tc.psum_pool(name="psum", bufs=1))
+
+        def bank(index, shape):
+            return psum.tile(shape, F32, tag="bank%d" % index, name="bank%d" % index)
 
         x_rows = keep.tile([P, PACK, PIXELS], BF16)
         nc.sync.dma_start(
@@ -77,15 +81,15 @@ def tile_psr4convf_kernel(tc, x, W, W1, out):
             in_=x_grouped[:].rearrange("q n t -> q (n t)"),
         )
 
-        def transpose_and_quantise(first, second, codes, scales):
-            bank = work.tile([P, 2, 2, P], F32, tag="work", name="bank")
+        def transpose_and_quantise(index, first, second, codes, scales):
+            turned = bank(index, [P, 2, 2, P])
             for a, words in enumerate((first, second)):
                 for u in range(2):
-                    nc.tensor.transpose(bank[:, a, u, :], words[:, u * P : (u + 1) * P], ident[:])
+                    nc.tensor.transpose(turned[:, a, u, :], words[:, u * P : (u + 1) * P], ident[:])
             grouped = stage.tile([P, 2 * P * PACK], BF16, align_bytes=64, name="grouped")
             nc.scalar.copy(
                 out=grouped[:].bitcast(F32).rearrange("q (a c u) -> q a c u", a=2, u=2),
-                in_=bank[:].rearrange("q a u c -> q a c u"),
+                in_=turned[:].rearrange("q a u c -> q a c u"),
             )
             nc.vector.quantize_mx(out=codes.bitcast(FP8X4), scales=scales, in_=grouped[:])
 
@@ -111,6 +115,7 @@ def tile_psr4convf_kernel(tc, x, W, W1, out):
             for k in range(NUM_K):
                 cols = slice(k * words_of_k, (k + 1) * words_of_k)
                 transpose_and_quantise(
+                    (pair * NUM_K + k) % BANKS,
                     w_by_k[2 * pair][:].bitcast(F32)[:, cols],
                     w_by_k[2 * pair + 1][:].bitcast(F32)[:, cols],
                     w_codes[:, pair, k, :],
@@ -125,7 +130,7 @@ def tile_psr4convf_kernel(tc, x, W, W1, out):
             centred = h_image[(0, slot)]
             half_pixels = PIXELS // 2
             for half in range(2):
-                z = work.tile([P, PACK, half_pixels], F32, tag="work", name="z")
+                z = bank(WORK_BANKS[half], [P, PACK, half_pixels])
                 pixels = slice(half * half_pixels, (half + 1) * half_pixels)
                 for t in range(TILES):
                     cols = slice((t % 2) * P, (t % 2 + 1) * P)
@@ -178,32 +183,38 @@ def tile_psr4convf_kernel(tc, x, W, W1, out):
 
         out_dram = out[0].rearrange("(a q) (s r) h w -> a s q (r h w)", q=P, s=2)
 
-        def store(total, a, pair):
+        def store(g, total, a, pair):
             result = stage.tile([P, 2 * PIXELS], F32, name="result")
-            nc.scalar.copy(out=result[:], in_=total[:])
+            if g % 2 == 0:
+                nc.scalar.copy(out=result[:], in_=total[:])
+            else:
+                nc.vector.tensor_copy(out=result[:], in_=total[:])
             nc.sync.dma_start(out=out_dram[a, pair], in_=result[:])
 
-        totals = []
-        for a in range(TILES):
-            total = sums.tile([P, 2 * PIXELS], F32, tag="sums", name="total")
-            totals.append(total)
-        for k in range(NUM_K):
+        def prepare(k):
+            words = w1_rows[k][:].bitcast(F32)
             for pair in range(TILES // 2):
-                words = w1_rows[k][:].bitcast(F32)
                 transpose_and_quantise(
+                    WORK_BANKS[pair],
                     words[:, 2 * pair * words_of_k : (2 * pair + 1) * words_of_k],
                     words[:, (2 * pair + 1) * words_of_k : (2 * pair + 2) * words_of_k],
                     w1_codes[:, pair, k, :],
                     w1_scales[:, pair, k, :],
                 )
             hidden_layer(k)
-            for a in range(TILES):
-                add_position(totals[a], a, k, 0)
-        for a in range(TILES):
-            store(totals[a], a, 0)
 
-        for a in range(TILES):
-            total = sums.tile([P, 2 * PIXELS], F32, tag="sums", name="total")
-            for k in range(NUM_K):
-                add_position(total, a, k, 1)
-            store(total, a, 1)
+        groups = [(a, pair) for pair in range(ROTATIONS // 2) for a in range(TILES)]
+        early = len(groups) - len(WORK_BANKS)
+        totals = [bank(g, [P, 2 * PIXELS]) for g in range(early)]
+        prepare(0)
+        for k in range(NUM_K - 1):
+            prepare(k + 1)
+            for g in range(early):
+                add_position(totals[g], groups[g][0], k, groups[g][1])
+        for g in range(early, len(groups)):
+            totals.append(bank(g, [P, 2 * PIXELS]))
+            for k in range(NUM_K - 1):
+                add_position(totals[g], groups[g][0], k, groups[g][1])
+        for g in range(len(groups)):
+            add_position(totals[g], groups[g][0], NUM_K - 1, groups[g][1])
+            store(g, totals[g], groups[g][0], groups[g][1])

@@ -22,7 +22,9 @@ ROTATIONS = 4
 RING = [(-1, -1), (-1, 0), (-1, 1), (0, 1), (1, 1), (1, 0), (1, -1), (0, -1)]
 PLANES = 3
 BANKS = 8
-WORK_BANKS = (6, 7)
+EARLY_GROUPS = 4
+WEIGHTS_LEAD = 3
+HIDDEN_LEAD = 2
 
 FLOPS = 2 * 2 * NUM_K * CH * CH * PIXELS
 
@@ -38,10 +40,10 @@ def tile_psr4convf_kernel(tc, x, W, W1, out):
         w_in = ctx.enter_context(tc.tile_pool(name="w_in", bufs=TILES))
         w1_in = ctx.enter_context(tc.tile_pool(name="w1_in", bufs=7))
         stage = ctx.enter_context(tc.tile_pool(name="stage", bufs=4))
-        psum = ctx.enter_context(tc.psum_pool(name="psum", bufs=1))
+        psum = ctx.enter_context(tc.psum_pool(name="psum", bufs=BANKS))
 
-        def bank(index, shape):
-            return psum.tile(shape, F32, tag="bank%d" % index, name="bank%d" % index)
+        def bank(shape):
+            return psum.tile(shape, F32, tag="bank", name="bank")
 
         x_rows = keep.tile([P, PACK, PIXELS], BF16)
         nc.sync.dma_start(
@@ -81,8 +83,8 @@ def tile_psr4convf_kernel(tc, x, W, W1, out):
             in_=x_grouped[:].rearrange("q n t -> q (n t)"),
         )
 
-        def transpose_and_quantise(index, first, second, codes, scales):
-            turned = bank(index, [P, 2, 2, P])
+        def transpose_and_quantise(first, second, codes, scales):
+            turned = bank([P, 2, 2, P])
             for a, words in enumerate((first, second)):
                 for u in range(2):
                     nc.tensor.transpose(turned[:, a, u, :], words[:, u * P : (u + 1) * P], ident[:])
@@ -93,33 +95,42 @@ def tile_psr4convf_kernel(tc, x, W, W1, out):
             )
             nc.vector.quantize_mx(out=codes.bitcast(FP8X4), scales=scales, in_=grouped[:])
 
-        w_by_k = []
-        for t in range(TILES):
-            planes = keep.tile([P, NUM_K * CH], BF16, name="w_by_k%d" % t)
-            for g in range(NUM_K // PLANES):
-                ks = slice(g * PLANES, (g + 1) * PLANES)
-                src = w_rows[t][:].rearrange("q (c k) -> q c k", k=NUM_K)[:, :, ks]
-                dst = planes[:].rearrange("q (k c) -> q c k", k=NUM_K)[:, :, ks]
-                if g < 2:
-                    nc.vector.tensor_copy(out=dst, in_=src)
-                else:
-                    nc.scalar.copy(out=dst, in_=src)
-            w_by_k.append(planes)
+        w_by_k = [keep.tile([P, NUM_K * CH], BF16, name="w_by_k%d" % t) for t in range(TILES)]
+
+        def take_apart(t, g):
+            ks = slice(g * PLANES, (g + 1) * PLANES)
+            src = w_rows[t][:].rearrange("q (c k) -> q c k", k=NUM_K)[:, :, ks]
+            dst = w_by_k[t][:].rearrange("q (k c) -> q c k", k=NUM_K)[:, :, ks]
+            if g < 2:
+                nc.vector.tensor_copy(out=dst, in_=src)
+            else:
+                nc.scalar.copy(out=dst, in_=src)
 
         w_codes = keep.tile([P, TILES // 2, NUM_K, 2 * P], U32, align_bytes=64)
         w_scales = keep.tile([P, TILES // 2, NUM_K, 2 * P], U8, align_bytes=64)
         w1_codes = keep.tile([P, TILES // 2, NUM_K, 2 * P], U32, align_bytes=64)
         w1_scales = keep.tile([P, TILES // 2, NUM_K, 2 * P], U8, align_bytes=64)
         words_of_k = CH // 2
-        for pair in range(TILES // 2):
-            for k in range(NUM_K):
-                cols = slice(k * words_of_k, (k + 1) * words_of_k)
+
+        def weights(k):
+            if k % PLANES == 0:
+                for t in range(TILES):
+                    take_apart(t, k // PLANES)
+            cols = slice(k * words_of_k, (k + 1) * words_of_k)
+            for pair in range(TILES // 2):
                 transpose_and_quantise(
-                    (pair * NUM_K + k) % BANKS,
                     w_by_k[2 * pair][:].bitcast(F32)[:, cols],
                     w_by_k[2 * pair + 1][:].bitcast(F32)[:, cols],
                     w_codes[:, pair, k, :],
                     w_scales[:, pair, k, :],
+                )
+            words = w1_rows[k][:].bitcast(F32)
+            for pair in range(TILES // 2):
+                transpose_and_quantise(
+                    words[:, 2 * pair * words_of_k : (2 * pair + 1) * words_of_k],
+                    words[:, (2 * pair + 1) * words_of_k : (2 * pair + 2) * words_of_k],
+                    w1_codes[:, pair, k, :],
+                    w1_scales[:, pair, k, :],
                 )
 
         h_codes = keep.tile([P, NUM_K, ROTATIONS // 2, 2 * PIXELS], U32, align_bytes=64)
@@ -130,7 +141,7 @@ def tile_psr4convf_kernel(tc, x, W, W1, out):
             centred = h_image[(0, slot)]
             half_pixels = PIXELS // 2
             for half in range(2):
-                z = bank(WORK_BANKS[half], [P, PACK, half_pixels])
+                z = bank([P, PACK, half_pixels])
                 pixels = slice(half * half_pixels, (half + 1) * half_pixels)
                 for t in range(TILES):
                     cols = slice((t % 2) * P, (t % 2 + 1) * P)
@@ -191,30 +202,23 @@ def tile_psr4convf_kernel(tc, x, W, W1, out):
                 nc.vector.tensor_copy(out=result[:], in_=total[:])
             nc.sync.dma_start(out=out_dram[a, pair], in_=result[:])
 
-        def prepare(k):
-            words = w1_rows[k][:].bitcast(F32)
-            for pair in range(TILES // 2):
-                transpose_and_quantise(
-                    WORK_BANKS[pair],
-                    words[:, 2 * pair * words_of_k : (2 * pair + 1) * words_of_k],
-                    words[:, (2 * pair + 1) * words_of_k : (2 * pair + 2) * words_of_k],
-                    w1_codes[:, pair, k, :],
-                    w1_scales[:, pair, k, :],
-                )
-            hidden_layer(k)
-
         groups = [(a, pair) for pair in range(ROTATIONS // 2) for a in range(TILES)]
-        early = len(groups) - len(WORK_BANKS)
-        totals = [bank(g, [P, 2 * PIXELS]) for g in range(early)]
-        prepare(0)
-        for k in range(NUM_K - 1):
-            prepare(k + 1)
-            for g in range(early):
+        totals = [bank([P, 2 * PIXELS]) for g in range(EARLY_GROUPS)]
+        for k in range(WEIGHTS_LEAD):
+            weights(k)
+        for k in range(HIDDEN_LEAD):
+            hidden_layer(k)
+        for k in range(NUM_K):
+            if k + WEIGHTS_LEAD < NUM_K:
+                weights(k + WEIGHTS_LEAD)
+            if k + HIDDEN_LEAD < NUM_K:
+                hidden_layer(k + HIDDEN_LEAD)
+            for g in range(EARLY_GROUPS):
                 add_position(totals[g], groups[g][0], k, groups[g][1])
-        for g in range(early, len(groups)):
-            totals.append(bank(g, [P, 2 * PIXELS]))
-            for k in range(NUM_K - 1):
-                add_position(totals[g], groups[g][0], k, groups[g][1])
-        for g in range(len(groups)):
-            add_position(totals[g], groups[g][0], NUM_K - 1, groups[g][1])
+        for g in range(EARLY_GROUPS):
             store(g, totals[g], groups[g][0], groups[g][1])
+        for g in range(EARLY_GROUPS, len(groups)):
+            total = bank([P, 2 * PIXELS])
+            for k in range(NUM_K):
+                add_position(total, groups[g][0], k, groups[g][1])
+            store(g, total, groups[g][0], groups[g][1])

@@ -160,8 +160,7 @@ def tile_psr4convf_kernel(tc, x, W, W1, out):
                     in_=z[:].rearrange("q t n -> q n t"),
                     func=RELU,
                 )
-            rotations = ROTATIONS // 2 if k == CENTRE else ROTATIONS
-            shifts = [shift_of(k, r) for r in range(rotations)]
+            shifts = [shift_of(k, r) for r in range(1 if k == CENTRE else ROTATIONS)]
             for dx in (-1, 1):
                 if any(s[1] == dx for s in shifts):
                     lo, hi = max(0, -dx), SIDE - max(0, dx)
@@ -181,25 +180,44 @@ def tile_psr4convf_kernel(tc, x, W, W1, out):
 
         def add_position(total, a, k, pair):
             cols = slice((a % 2) * P, (a % 2 + 1) * P)
-            h_pair = 0 if k == CENTRE else pair
             nc.tensor.matmul_mx(
                 out=total[:],
                 lhsT=w1_codes[:, a // 2, k, cols].bitcast(FP8X4),
                 lhsT_scale=w1_scales[:, a // 2, k, cols],
-                rhs=h_codes[:, k, h_pair, :].bitcast(FP8X4),
-                rhs_scale=h_scales[:, k, h_pair, :],
+                rhs=h_codes[:, k, pair, :].bitcast(FP8X4),
+                rhs_scale=h_scales[:, k, pair, :],
                 start=(k == 0),
-                stop=(k == NUM_K - 1),
+                stop=(k == CENTRE - 1),
             )
+
+        centre = keep.tile([P, TILES, PIXELS], F32)
+
+        def centre_product():
+            for pair in range(TILES // 2):
+                product = bank([P, 2, PIXELS])
+                for half in range(2):
+                    cols = slice(half * P, (half + 1) * P)
+                    nc.tensor.matmul_mx(
+                        out=product[:, half, :],
+                        lhsT=w1_codes[:, pair, CENTRE, cols].bitcast(FP8X4),
+                        lhsT_scale=w1_scales[:, pair, CENTRE, cols],
+                        rhs=h_codes[:, CENTRE, 0, 0:PIXELS].bitcast(FP8X4),
+                        rhs_scale=h_scales[:, CENTRE, 0, 0:PIXELS],
+                        start=True,
+                        stop=True,
+                    )
+                nc.scalar.copy(out=centre[:, 2 * pair : 2 * pair + 2, :], in_=product[:])
 
         out_dram = out[0].rearrange("(a q) (s r) h w -> a s q (r h w)", q=P, s=2)
 
-        def store(g, total, a, pair):
+        def store(total, a, pair):
             result = stage.tile([P, 2 * PIXELS], F32, name="result")
-            if g % 2 == 0:
-                nc.scalar.copy(out=result[:], in_=total[:])
-            else:
-                nc.vector.tensor_copy(out=result[:], in_=total[:])
+            nc.vector.tensor_tensor(
+                out=result[:].rearrange("q (r n) -> q r n", r=2),
+                in0=total[:].rearrange("q (r n) -> q r n", r=2),
+                in1=centre[:, a, :].unsqueeze(1).to_broadcast([P, 2, PIXELS]),
+                op=mybir.AluOpType.add,
+            )
             nc.sync.dma_start(out=out_dram[a, pair], in_=result[:])
 
         groups = [(a, pair) for pair in range(ROTATIONS // 2) for a in range(TILES)]
@@ -213,12 +231,15 @@ def tile_psr4convf_kernel(tc, x, W, W1, out):
                 weights(k + WEIGHTS_LEAD)
             if k + HIDDEN_LEAD < NUM_K:
                 hidden_layer(k + HIDDEN_LEAD)
-            for g in range(EARLY_GROUPS):
-                add_position(totals[g], groups[g][0], k, groups[g][1])
+            if k == CENTRE:
+                centre_product()
+            else:
+                for g in range(EARLY_GROUPS):
+                    add_position(totals[g], groups[g][0], k, groups[g][1])
         for g in range(EARLY_GROUPS):
-            store(g, totals[g], groups[g][0], groups[g][1])
+            store(totals[g], groups[g][0], groups[g][1])
         for g in range(EARLY_GROUPS, len(groups)):
             total = bank([P, 2 * PIXELS])
-            for k in range(NUM_K):
+            for k in range(CENTRE):
                 add_position(total, groups[g][0], k, groups[g][1])
-            store(g, total, groups[g][0], groups[g][1])
+            store(total, groups[g][0], groups[g][1])

@@ -14,6 +14,7 @@ P = 128
 PACK = 4
 CH = 512
 TILES = CH // P
+PAIRS = TILES // 2
 NUM_K = 9
 CENTRE = 8
 SIDE = 16
@@ -22,15 +23,9 @@ ROTATIONS = 4
 RING = [(-1, -1), (-1, 0), (-1, 1), (0, 1), (1, 1), (1, 0), (1, -1), (0, -1)]
 PLANES = 3
 BANKS = 8
-EARLY_GROUPS = 4
-WEIGHTS_LEAD = 3
-HIDDEN_LEAD = 2
+TURN_LEAD = 4
 
 FLOPS = 2 * 2 * NUM_K * CH * CH * PIXELS
-
-
-def shift_of(k, r):
-    return (0, 0) if k == CENTRE else RING[(k + 2 * r) % len(RING)]
 
 
 def tile_psr4convf_kernel(tc, x, W, W1, out):
@@ -38,8 +33,9 @@ def tile_psr4convf_kernel(tc, x, W, W1, out):
     with ExitStack() as ctx:
         keep = ctx.enter_context(tc.tile_pool(name="keep", bufs=1))
         w_in = ctx.enter_context(tc.tile_pool(name="w_in", bufs=TILES))
-        w1_in = ctx.enter_context(tc.tile_pool(name="w1_in", bufs=7))
-        stage = ctx.enter_context(tc.tile_pool(name="stage", bufs=4))
+        w1_in = ctx.enter_context(tc.tile_pool(name="w1_in", bufs=5))
+        turned_out = ctx.enter_context(tc.tile_pool(name="turned_out", bufs=8))
+        results = ctx.enter_context(tc.tile_pool(name="results", bufs=4))
         psum = ctx.enter_context(tc.psum_pool(name="psum", bufs=BANKS))
 
         def bank(shape):
@@ -83,18 +79,6 @@ def tile_psr4convf_kernel(tc, x, W, W1, out):
             in_=x_grouped[:].rearrange("q n t -> q (n t)"),
         )
 
-        def transpose_and_quantise(first, second, codes, scales):
-            turned = bank([P, 2, 2, P])
-            for a, words in enumerate((first, second)):
-                for u in range(2):
-                    nc.tensor.transpose(turned[:, a, u, :], words[:, u * P : (u + 1) * P], ident[:])
-            grouped = stage.tile([P, 2 * P * PACK], BF16, align_bytes=64, name="grouped")
-            nc.scalar.copy(
-                out=grouped[:].bitcast(F32).rearrange("q (a c u) -> q a c u", a=2, u=2),
-                in_=turned[:].rearrange("q a u c -> q a c u"),
-            )
-            nc.vector.quantize_mx(out=codes.bitcast(FP8X4), scales=scales, in_=grouped[:])
-
         w_by_k = [keep.tile([P, NUM_K * CH], BF16, name="w_by_k%d" % t) for t in range(TILES)]
 
         def take_apart(t, g):
@@ -106,39 +90,46 @@ def tile_psr4convf_kernel(tc, x, W, W1, out):
             else:
                 nc.scalar.copy(out=dst, in_=src)
 
-        w_codes = keep.tile([P, TILES // 2, NUM_K, 2 * P], U32, align_bytes=64)
-        w_scales = keep.tile([P, TILES // 2, NUM_K, 2 * P], U8, align_bytes=64)
-        w1_codes = keep.tile([P, TILES // 2, NUM_K, 2 * P], U32, align_bytes=64)
-        w1_scales = keep.tile([P, TILES // 2, NUM_K, 2 * P], U8, align_bytes=64)
+        shape = [P, PAIRS, NUM_K, 2 * P]
+        codes_of = {
+            "w": keep.tile(shape, U32, align_bytes=64, name="w_codes"),
+            "w1": keep.tile(shape, U32, align_bytes=64, name="w1_codes"),
+        }
+        scales_of = {
+            "w": keep.tile(shape, U8, align_bytes=64, name="w_scales"),
+            "w1": keep.tile(shape, U8, align_bytes=64, name="w1_scales"),
+        }
         words_of_k = CH // 2
+        grouped_of = {}
 
-        def weights(k):
-            if k % PLANES == 0:
-                for t in range(TILES):
-                    take_apart(t, k // PLANES)
-            cols = slice(k * words_of_k, (k + 1) * words_of_k)
-            for pair in range(TILES // 2):
-                transpose_and_quantise(
-                    w_by_k[2 * pair][:].bitcast(F32)[:, cols],
-                    w_by_k[2 * pair + 1][:].bitcast(F32)[:, cols],
-                    w_codes[:, pair, k, :],
-                    w_scales[:, pair, k, :],
-                )
-            words = w1_rows[k][:].bitcast(F32)
-            for pair in range(TILES // 2):
-                transpose_and_quantise(
-                    words[:, 2 * pair * words_of_k : (2 * pair + 1) * words_of_k],
-                    words[:, (2 * pair + 1) * words_of_k : (2 * pair + 2) * words_of_k],
-                    w1_codes[:, pair, k, :],
-                    w1_scales[:, pair, k, :],
-                )
+        def turn(which, pair, k):
+            turned = bank([P, 2, 2, P])
+            for a in range(2):
+                if which == "w":
+                    words = w_by_k[2 * pair + a][:].bitcast(F32)[:, k * words_of_k : (k + 1) * words_of_k]
+                else:
+                    first = (2 * pair + a) * words_of_k
+                    words = w1_rows[k][:].bitcast(F32)[:, first : first + words_of_k]
+                for u in range(2):
+                    nc.tensor.transpose(turned[:, a, u, :], words[:, u * P : (u + 1) * P], ident[:])
+            grouped = turned_out.tile([P, 2 * P * PACK], BF16, align_bytes=64, name="grouped")
+            nc.scalar.copy(
+                out=grouped[:].bitcast(F32).rearrange("q (a c u) -> q a c u", a=2, u=2),
+                in_=turned[:].rearrange("q a u c -> q a c u"),
+            )
+            grouped_of[(which, pair, k)] = grouped
+
+        def quantise(which, pair, k):
+            nc.vector.quantize_mx(
+                out=codes_of[which][:, pair, k, :].bitcast(FP8X4),
+                scales=scales_of[which][:, pair, k, :],
+                in_=grouped_of[(which, pair, k)][:],
+            )
 
         h_codes = keep.tile([P, NUM_K, ROTATIONS // 2, 2 * PIXELS], U32, align_bytes=64)
         h_scales = keep.tile([P, NUM_K, ROTATIONS // 2, 2 * PIXELS], U8, align_bytes=64)
 
         def hidden_layer(k):
-            slot = k % 2
-            centred = h_image[(0, slot)]
             half_pixels = PIXELS // 2
             for half in range(2):
                 z = bank([P, PACK, half_pixels])
@@ -147,8 +138,8 @@ def tile_psr4convf_kernel(tc, x, W, W1, out):
                     cols = slice((t % 2) * P, (t % 2 + 1) * P)
                     nc.tensor.matmul_mx(
                         out=z[:, t, :],
-                        lhsT=w_codes[:, t // 2, k, cols].bitcast(FP8X4),
-                        lhsT_scale=w_scales[:, t // 2, k, cols],
+                        lhsT=codes_of["w"][:, t // 2, k, cols].bitcast(FP8X4),
+                        lhsT_scale=scales_of["w"][:, t // 2, k, cols],
                         rhs=x_codes[:, pixels].bitcast(FP8X4),
                         rhs_scale=x_scales[:, pixels],
                         start=True,
@@ -156,20 +147,32 @@ def tile_psr4convf_kernel(tc, x, W, W1, out):
                     )
                 begin = (SIDE + half * half_pixels) * PACK
                 nc.scalar.activation(
-                    out=centred[:, begin : begin + half_pixels * PACK].rearrange("q (n t) -> q n t", t=PACK),
+                    out=h_image[(0, k % 2)][:, begin : begin + half_pixels * PACK].rearrange(
+                        "q (n t) -> q n t", t=PACK
+                    ),
                     in_=z[:].rearrange("q t n -> q n t"),
                     func=RELU,
                 )
-            shifts = [shift_of(k, r) for r in range(1 if k == CENTRE else ROTATIONS)]
+
+        def shifts_of(k):
+            if k == CENTRE:
+                return [(0, 0)]
+            return [RING[(k + 2 * r) % len(RING)] for r in range(ROTATIONS)]
+
+        def shift_columns(k):
+            slot = k % 2
             for dx in (-1, 1):
-                if any(s[1] == dx for s in shifts):
+                if any(s[1] == dx for s in shifts_of(k)):
                     lo, hi = max(0, -dx), SIDE - max(0, dx)
-                    src = centred[:].rearrange("q (i j t) -> q i j t", j=SIDE, t=PACK)
+                    src = h_image[(0, slot)][:].rearrange("q (i j t) -> q i j t", j=SIDE, t=PACK)
                     dst = h_image[(dx, slot)][:].rearrange("q (i j t) -> q i j t", j=SIDE, t=PACK)
                     nc.vector.tensor_copy(
                         out=dst[:, 1 : SIDE + 1, lo:hi, :], in_=src[:, 1 : SIDE + 1, lo + dx : hi + dx, :]
                     )
-            for r, (dy, dx) in enumerate(shifts):
+
+        def quantise_hidden(k):
+            slot = k % 2
+            for r, (dy, dx) in enumerate(shifts_of(k)):
                 begin = (1 + dy) * SIDE * PACK
                 cols = slice((r % 2) * PIXELS, (r % 2 + 1) * PIXELS)
                 nc.vector.quantize_mx(
@@ -178,14 +181,14 @@ def tile_psr4convf_kernel(tc, x, W, W1, out):
                     in_=h_image[(dx, slot)][:, begin : begin + PIXELS * PACK],
                 )
 
-        def add_position(total, a, k, pair):
+        def add_position(total, a, k, rotations):
             cols = slice((a % 2) * P, (a % 2 + 1) * P)
             nc.tensor.matmul_mx(
                 out=total[:],
-                lhsT=w1_codes[:, a // 2, k, cols].bitcast(FP8X4),
-                lhsT_scale=w1_scales[:, a // 2, k, cols],
-                rhs=h_codes[:, k, pair, :].bitcast(FP8X4),
-                rhs_scale=h_scales[:, k, pair, :],
+                lhsT=codes_of["w1"][:, a // 2, k, cols].bitcast(FP8X4),
+                lhsT_scale=scales_of["w1"][:, a // 2, k, cols],
+                rhs=h_codes[:, k, rotations, :].bitcast(FP8X4),
+                rhs_scale=h_scales[:, k, rotations, :],
                 start=(k == 0),
                 stop=(k == CENTRE - 1),
             )
@@ -193,14 +196,14 @@ def tile_psr4convf_kernel(tc, x, W, W1, out):
         centre = keep.tile([P, TILES, PIXELS], F32)
 
         def centre_product():
-            for pair in range(TILES // 2):
+            for pair in range(PAIRS):
                 product = bank([P, 2, PIXELS])
-                for half in range(2):
-                    cols = slice(half * P, (half + 1) * P)
+                for a in range(2):
+                    cols = slice(a * P, (a + 1) * P)
                     nc.tensor.matmul_mx(
-                        out=product[:, half, :],
-                        lhsT=w1_codes[:, pair, CENTRE, cols].bitcast(FP8X4),
-                        lhsT_scale=w1_scales[:, pair, CENTRE, cols],
+                        out=product[:, a, :],
+                        lhsT=codes_of["w1"][:, pair, CENTRE, cols].bitcast(FP8X4),
+                        lhsT_scale=scales_of["w1"][:, pair, CENTRE, cols],
                         rhs=h_codes[:, CENTRE, 0, 0:PIXELS].bitcast(FP8X4),
                         rhs_scale=h_scales[:, CENTRE, 0, 0:PIXELS],
                         start=True,
@@ -210,36 +213,71 @@ def tile_psr4convf_kernel(tc, x, W, W1, out):
 
         out_dram = out[0].rearrange("(a q) (s r) h w -> a s q (r h w)", q=P, s=2)
 
-        def store(total, a, pair):
-            result = stage.tile([P, 2 * PIXELS], F32, name="result")
+        def store(total, a, rotations):
+            result = results.tile([P, 2 * PIXELS], F32, name="result")
             nc.vector.tensor_tensor(
                 out=result[:].rearrange("q (r n) -> q r n", r=2),
                 in0=total[:].rearrange("q (r n) -> q r n", r=2),
                 in1=centre[:, a, :].unsqueeze(1).to_broadcast([P, 2, PIXELS]),
                 op=mybir.AluOpType.add,
             )
-            nc.sync.dma_start(out=out_dram[a, pair], in_=result[:])
+            nc.sync.dma_start(out=out_dram[a, rotations], in_=result[:])
 
-        groups = [(a, pair) for pair in range(ROTATIONS // 2) for a in range(TILES)]
-        totals = [bank([P, 2 * PIXELS]) for g in range(EARLY_GROUPS)]
-        for k in range(WEIGHTS_LEAD):
-            weights(k)
-        for k in range(HIDDEN_LEAD):
+        late = (("w", 1), ("w1", 0), ("w1", 1))
+        for t in range(2):
+            for g in range(NUM_K // PLANES):
+                take_apart(t, g)
+        for t in range(2, TILES):
+            take_apart(t, 0)
+        for k in range(2):
+            turn("w", 0, k)
+            quantise("w", 0, k)
+            for which, pair in late:
+                turn(which, pair, k)
+                quantise(which, pair, k)
             hidden_layer(k)
+        shift_columns(0)
+        quantise_hidden(0)
+        for t in range(2, TILES):
+            take_apart(t, 1)
+        for k in range(2, TURN_LEAD):
+            turn("w", 0, k)
+            quantise("w", 0, k)
+            for which, pair in late:
+                turn(which, pair, k)
+        for which, pair in late:
+            quantise(which, pair, 2)
+        for t in range(2, TILES):
+            take_apart(t, 2)
+        for k in range(TURN_LEAD, NUM_K):
+            turn("w", 0, k)
+            quantise("w", 0, k)
+
+        ctx.enter_context(tc.manual_schedule())
+        totals = [bank([P, 2 * PIXELS]) for a in range(TILES)]
         for k in range(NUM_K):
-            if k + WEIGHTS_LEAD < NUM_K:
-                weights(k + WEIGHTS_LEAD)
-            if k + HIDDEN_LEAD < NUM_K:
-                hidden_layer(k + HIDDEN_LEAD)
+            if k + TURN_LEAD < NUM_K:
+                for which, pair in late:
+                    turn(which, pair, k + TURN_LEAD)
+            if k + 1 < NUM_K:
+                shift_columns(k + 1)
+            if k + TURN_LEAD - 1 < NUM_K:
+                for which, pair in late:
+                    quantise(which, pair, k + TURN_LEAD - 1)
+            if k + 1 < NUM_K:
+                quantise_hidden(k + 1)
+            if k + 2 < NUM_K:
+                hidden_layer(k + 2)
             if k == CENTRE:
                 centre_product()
             else:
-                for g in range(EARLY_GROUPS):
-                    add_position(totals[g], groups[g][0], k, groups[g][1])
-        for g in range(EARLY_GROUPS):
-            store(totals[g], groups[g][0], groups[g][1])
-        for g in range(EARLY_GROUPS, len(groups)):
+                for a in range(TILES):
+                    add_position(totals[a], a, k, 0)
+        for a in range(TILES):
+            store(totals[a], a, 0)
+
+        for a in range(TILES):
             total = bank([P, 2 * PIXELS])
             for k in range(CENTRE):
-                add_position(total, groups[g][0], k, groups[g][1])
-            store(total, groups[g][0], groups[g][1])
+                add_position(total, a, k, 1)
+            store(total, a, 1)

from contextlib import ExitStack

import concourse.masks as masks
import concourse.mybir as mybir

BF16 = mybir.dt.bfloat16
F32 = mybir.dt.float32
U32 = mybir.dt.uint32
U8 = mybir.dt.uint8
FP8X4 = mybir.dt.float8_e4m3fn_x4
RELU = mybir.ActivationFunctionType.Relu

P = 128
PACK = 4
CH = 512
TILES = CH // P
PAIRS = TILES // 2
NUM_K = 9
CENTRE = 8
SIDE = 16
PIXELS = SIDE * SIDE
ROTATIONS = 4
RING = [(-1, -1), (-1, 0), (-1, 1), (0, 1), (1, 1), (1, 0), (1, -1), (0, -1)]
PLANES = 3
BANKS = 8
TURN_LEAD = 4

FLOPS = 2 * 2 * NUM_K * CH * CH * PIXELS


def tile_psr4convf_kernel(tc, x, W, W1, out):
    nc = tc.nc
    with ExitStack() as ctx:
        keep = ctx.enter_context(tc.tile_pool(name="keep", bufs=1))
        w_in = ctx.enter_context(tc.tile_pool(name="w_in", bufs=TILES))
        w1_in = ctx.enter_context(tc.tile_pool(name="w1_in", bufs=5))
        turned_out = ctx.enter_context(tc.tile_pool(name="turned_out", bufs=8))
        results = ctx.enter_context(tc.tile_pool(name="results", bufs=4))
        psum = ctx.enter_context(tc.psum_pool(name="psum", bufs=BANKS))

        def bank(shape):
            return psum.tile(shape, F32, tag="bank", name="bank")

        x_rows = keep.tile([P, PACK, PIXELS], BF16)
        nc.sync.dma_start(
            out=x_rows[:].rearrange("q (u e) n -> q u e n", u=2),
            in_=x[0].rearrange("(u q e) h w -> q u e (h w)", u=2, e=2),
        )
        w_dram = W.rearrange("(u q e) c k -> u e q (c k)", u=2, e=2)
        w_rows = []
        for t in range(TILES):
            rows = w_in.tile([P, CH * NUM_K], BF16, name="w_rows")
            nc.sync.dma_start(out=rows[:], in_=w_dram[t // 2, t % 2])
            w_rows.append(rows)
        w1_dram = W1.rearrange("(a q) (k o) -> k q a o", q=P, k=NUM_K)
        w1_rows = []
        for k in range(NUM_K):
            rows = w1_in.tile([P, TILES * CH], BF16, name="w1_rows")
            nc.sync.dma_start(out=rows[:].rearrange("q (a o) -> q a o", a=TILES), in_=w1_dram[k])
            w1_rows.append(rows)

        ident = keep.tile([P, P], F32)
        masks.make_identity(nc, ident[:])
        padded = (SIDE + 2) * SIDE * PACK
        h_image = {}
        for dx in (-1, 0, 1):
            for slot in range(2):
                image = keep.tile([P, padded], BF16, align_bytes=64, name="h_image_%d_%d" % (dx + 1, slot))
                nc.vector.memset(image[:], 0.0)
                h_image[(dx, slot)] = image

        x_grouped = keep.tile([P, PIXELS, PACK], BF16, align_bytes=64)
        x_codes = keep.tile([P, PIXELS], U32, align_bytes=64)
        x_scales = keep.tile([P, PIXELS], U8, align_bytes=64)
        nc.vector.tensor_copy(out=x_grouped[:], in_=x_rows[:].rearrange("q t n -> q n t"))
        nc.vector.quantize_mx(
            out=x_codes[:].bitcast(FP8X4),
            scales=x_scales[:],
            in_=x_grouped[:].rearrange("q n t -> q (n t)"),
        )

        w_by_k = [keep.tile([P, NUM_K * CH], BF16, name="w_by_k%d" % t) for t in range(TILES)]

        def take_apart(t, g):
            ks = slice(g * PLANES, (g + 1) * PLANES)
            src = w_rows[t][:].rearrange("q (c k) -> q c k", k=NUM_K)[:, :, ks]
            dst = w_by_k[t][:].rearrange("q (k c) -> q c k", k=NUM_K)[:, :, ks]
            if g < 2:
                nc.vector.tensor_copy(out=dst, in_=src)
            else:
                nc.scalar.copy(out=dst, in_=src)

        shape = [P, PAIRS, NUM_K, 2 * P]
        codes_of = {
            "w": keep.tile(shape, U32, align_bytes=64, name="w_codes"),
            "w1": keep.tile(shape, U32, align_bytes=64, name="w1_codes"),
        }
        scales_of = {
            "w": keep.tile(shape, U8, align_bytes=64, name="w_scales"),
            "w1": keep.tile(shape, U8, align_bytes=64, name="w1_scales"),
        }
        words_of_k = CH // 2
        grouped_of = {}

        def turn(which, pair, k):
            turned = bank([P, 2, 2, P])
            for a in range(2):
                if which == "w":
                    words = w_by_k[2 * pair + a][:].bitcast(F32)[:, k * words_of_k : (k + 1) * words_of_k]
                else:
                    first = (2 * pair + a) * words_of_k
                    words = w1_rows[k][:].bitcast(F32)[:, first : first + words_of_k]
                for u in range(2):
                    nc.tensor.transpose(turned[:, a, u, :], words[:, u * P : (u + 1) * P], ident[:])
            grouped = turned_out.tile([P, 2 * P * PACK], BF16, align_bytes=64, name="grouped")
            nc.scalar.copy(
                out=grouped[:].bitcast(F32).rearrange("q (a c u) -> q a c u", a=2, u=2),
                in_=turned[:].rearrange("q a u c -> q a c u"),
            )
            grouped_of[(which, pair, k)] = grouped

        def quantise(which, pair, k):
            nc.vector.quantize_mx(
                out=codes_of[which][:, pair, k, :].bitcast(FP8X4),
                scales=scales_of[which][:, pair, k, :],
                in_=grouped_of[(which, pair, k)][:],
            )

        h_codes = keep.tile([P, NUM_K, ROTATIONS // 2, 2 * PIXELS], U32, align_bytes=64)
        h_scales = keep.tile([P, NUM_K, ROTATIONS // 2, 2 * PIXELS], U8, align_bytes=64)

        def hidden_layer(k):
            half_pixels = PIXELS // 2
            for half in range(2):
                z = bank([P, PACK, half_pixels])
                pixels = slice(half * half_pixels, (half + 1) * half_pixels)
                for t in range(TILES):
                    cols = slice((t % 2) * P, (t % 2 + 1) * P)
                    nc.tensor.matmul_mx(
                        out=z[:, t, :],
                        lhsT=codes_of["w"][:, t // 2, k, cols].bitcast(FP8X4),
                        lhsT_scale=scales_of["w"][:, t // 2, k, cols],
                        rhs=x_codes[:, pixels].bitcast(FP8X4),
                        rhs_scale=x_scales[:, pixels],
                        start=True,
                        stop=True,
                    )
                begin = (SIDE + half * half_pixels) * PACK
                nc.scalar.activation(
                    out=h_image[(0, k % 2)][:, begin : begin + half_pixels * PACK].rearrange(
                        "q (n t) -> q n t", t=PACK
                    ),
                    in_=z[:].rearrange("q t n -> q n t"),
                    func=RELU,
                )

        def shifts_of(k):
            if k == CENTRE:
                return [(0, 0)]
            return [RING[(k + 2 * r) % len(RING)] for r in range(ROTATIONS)]

        def shift_columns(k):
            slot = k % 2
            for dx in (-1, 1):
                if any(s[1] == dx for s in shifts_of(k)):
                    lo, hi = max(0, -dx), SIDE - max(0, dx)
                    src = h_image[(0, slot)][:].rearrange("q (i j t) -> q i j t", j=SIDE, t=PACK)
                    dst = h_image[(dx, slot)][:].rearrange("q (i j t) -> q i j t", j=SIDE, t=PACK)
                    nc.vector.tensor_copy(
                        out=dst[:, 1 : SIDE + 1, lo:hi, :], in_=src[:, 1 : SIDE + 1, lo + dx : hi + dx, :]
                    )

        def quantise_hidden(k):
            slot = k % 2
            for r, (dy, dx) in enumerate(shifts_of(k)):
                begin = (1 + dy) * SIDE * PACK
                cols = slice((r % 2) * PIXELS, (r % 2 + 1) * PIXELS)
                nc.vector.quantize_mx(
                    out=h_codes[:, k, r // 2, cols].bitcast(FP8X4),
                    scales=h_scales[:, k, r // 2, cols],
                    in_=h_image[(dx, slot)][:, begin : begin + PIXELS * PACK],
                )

        def add_position(total, a, k, rotations):
            cols = slice((a % 2) * P, (a % 2 + 1) * P)
            nc.tensor.matmul_mx(
                out=total[:],
                lhsT=codes_of["w1"][:, a // 2, k, cols].bitcast(FP8X4),
                lhsT_scale=scales_of["w1"][:, a // 2, k, cols],
                rhs=h_codes[:, k, rotations, :].bitcast(FP8X4),
                rhs_scale=h_scales[:, k, rotations, :],
                start=(k == 0),
                stop=(k == CENTRE - 1),
            )

        centre = keep.tile([P, TILES, PIXELS], F32)

        def centre_product():
            for pair in range(PAIRS):
                product = bank([P, 2, PIXELS])
                for a in range(2):
                    cols = slice(a * P, (a + 1) * P)
                    nc.tensor.matmul_mx(
                        out=product[:, a, :],
                        lhsT=codes_of["w1"][:, pair, CENTRE, cols].bitcast(FP8X4),
                        lhsT_scale=scales_of["w1"][:, pair, CENTRE, cols],
                        rhs=h_codes[:, CENTRE, 0, 0:PIXELS].bitcast(FP8X4),
                        rhs_scale=h_scales[:, CENTRE, 0, 0:PIXELS],
                        start=True,
                        stop=True,
                    )
                nc.scalar.copy(out=centre[:, 2 * pair : 2 * pair + 2, :], in_=product[:])

        out_dram = out[0].rearrange("(a q) (s r) h w -> a s q (r h w)", q=P, s=2)

        def store(total, a, rotations):
            result = results.tile([P, 2 * PIXELS], F32, name="result")
            nc.vector.tensor_tensor(
                out=result[:].rearrange("q (r n) -> q r n", r=2),
                in0=total[:].rearrange("q (r n) -> q r n", r=2),
                in1=centre[:, a, :].unsqueeze(1).to_broadcast([P, 2, PIXELS]),
                op=mybir.AluOpType.add,
            )
            nc.sync.dma_start(out=out_dram[a, rotations], in_=result[:])

        late = (("w", 1), ("w1", 0), ("w1", 1))
        for t in range(2):
            for g in range(NUM_K // PLANES):
                take_apart(t, g)
        for t in range(2, TILES):
            take_apart(t, 0)
        for k in range(2):
            turn("w", 0, k)
            quantise("w", 0, k)
            for which, pair in late:
                turn(which, pair, k)
                quantise(which, pair, k)
            hidden_layer(k)
        shift_columns(0)
        quantise_hidden(0)
        for t in range(2, TILES):
            take_apart(t, 1)
        for k in range(2, TURN_LEAD):
            turn("w", 0, k)
            quantise("w", 0, k)
            for which, pair in late:
                turn(which, pair, k)
        for which, pair in late:
            quantise(which, pair, 2)
        for t in range(2, TILES):
            take_apart(t, 2)
        for k in range(TURN_LEAD, NUM_K):
            turn("w", 0, k)
            quantise("w", 0, k)

        ctx.enter_context(tc.manual_schedule())
        totals = [bank([P, 2 * PIXELS]) for a in range(TILES)]
        for k in range(NUM_K):
            if k + TURN_LEAD < NUM_K:
                for which, pair in late:
                    turn(which, pair, k + TURN_LEAD)
            if k + 1 < NUM_K:
                shift_columns(k + 1)
            if k + TURN_LEAD - 1 < NUM_K:
                for which, pair in late:
                    quantise(which, pair, k + TURN_LEAD - 1)
            if k + 1 < NUM_K:
                quantise_hidden(k + 1)
            if k + 2 < NUM_K:
                hidden_layer(k + 2)
            if k == CENTRE:
                centre_product()
            else:
                for a in range(TILES):
                    add_position(totals[a], a, k, 0)
        for a in range(TILES):
            store(totals[a], a, 0)

        for a in range(TILES):
            total = bank([P, 2 * PIXELS])
            for k in range(CENTRE):
                add_position(total, a, k, 1)
            store(total, a, 1)
